import numpy as np
import ml_dtypes


def mxq(x, axis, fmt="e4m3"):
    dtype, down = {"e4m3": (ml_dtypes.float8_e4m3fn, 7), "e5m2": (ml_dtypes.float8_e5m2, 14)}[fmt]
    v = np.moveaxis(np.asarray(x, np.float32).astype(ml_dtypes.bfloat16).astype(np.float64), axis, -1)
    blocks = v.reshape(v.shape[:-1] + (-1, 32))
    amax = np.abs(blocks).max(-1, keepdims=True)
    byte = np.maximum(np.where(amax > 0, np.frexp(amax)[1] - 1 + 127, 0) - down, 1)
    scale = np.exp2(byte - 127.0)
    codes = (blocks / scale).astype(np.float32).astype(dtype).astype(np.float64)
    return np.moveaxis((codes * scale).reshape(v.shape), -1, axis)


WIDE = False


def mx_kscale(k):
    if not WIDE:
        return np.ones(k)
    levels = np.array([10, -10, 5, -5, 0])
    if k % 512:
        return np.exp2(np.random.permutation(np.resize(levels, k // 32))).repeat(32)
    a = np.empty((k // 512, 16))
    for p in range(k // 512):
        a[p, :8] = np.random.permutation(np.resize(levels, 8))
        for g in range(8):
            far = levels[np.abs(levels - a[p, g]) >= 10]
            a[p, g + 8] = far[np.random.randint(len(far))]
    return np.exp2(a.ravel()).repeat(32)


BF16 = ml_dtypes.bfloat16


def bf(x):
    return np.asarray(x, np.float32).astype(BF16)


def f64(x):
    return np.asarray(x).astype(np.float64)


B, T, S, Dt, Df = 2, 512, 512, 2048, 2048
EPS = 1e-6


def rmsnorm(x, w):
    return x * (1.0 / np.sqrt(np.mean(x * x, axis=-1, keepdims=True) + EPS)) * w


def setup_inputs():
    s = mx_kscale(Df)
    return {"features": bf(np.random.standard_normal((B, S, Df))),
            "fn_w": bf((1.0 + 0.1 * np.random.standard_normal(Df)) * s),
            "Wk_w": bf(np.random.standard_normal((Df, Df)) / np.sqrt(Df) / s[None, :]),
            "Wk_b": bf(np.random.standard_normal(Df) * 0.3),
            "kn_w": bf(1.0 + 0.1 * np.random.standard_normal(Df))}


def reference(features, fn_w, Wk_w, Wk_b, kn_w):
    features_n = rmsnorm(f64(features), f64(fn_w))
    k = (mxq(features_n, 2, "e4m3") @ mxq(f64(Wk_w), 1, "e4m3").T) + f64(Wk_b)
    return rmsnorm(k, f64(kn_w))

@@ -1,0 +1,203 @@
+from contextlib import ExitStack
+
+import concourse.mybir as mybir
+from concourse.masks import make_identity
+
+F32 = mybir.dt.float32
+BF16 = mybir.dt.bfloat16
+U32 = mybir.dt.uint32
+U8 = mybir.dt.uint8
+I32 = mybir.dt.int32
+FP8X4 = mybir.dt.float8_e4m3fn_x4
+ALU = mybir.AluOpType
+ACT = mybir.ActivationFunctionType
+
+P = 128
+TOKENS = 1024
+D = 2048
+EPS = 1e-6
+PACK = 4
+K_PASS = P * PACK
+PASSES = D // K_PASS
+WORDS = D // 2
+CHUNK = 512
+CHUNKS = D // CHUNK
+W_TILES_PER_CHUNK = CHUNK // P
+TOKEN_TILES = TOKENS // P
+EARLY = 4
+
+FLOPS = 2 * TOKENS * D * D
+
+
+def tile_crossattention_pa_kernel(tc, features, fn_w, Wk_w, Wk_b, kn_w, out):
+    nc = tc.nc
+    x_rows = features.flatten_outer_dims()
+    out_rows = out.flatten_outer_dims()
+
+    with ExitStack() as ctx:
+        const = ctx.enter_context(tc.tile_pool(name="const", bufs=1))
+        keep = ctx.enter_context(tc.tile_pool(name="keep", bufs=1))
+        x_in = ctx.enter_context(tc.tile_pool(name="x_in", bufs=4))
+        w_in = ctx.enter_context(tc.tile_pool(name="w_in", bufs=6))
+        work = ctx.enter_context(tc.tile_pool(name="work", bufs=2))
+        k_pool = ctx.enter_context(tc.tile_pool(name="k_pool", bufs=EARLY + 2))
+        psum = ctx.enter_context(tc.psum_pool(name="psum", bufs=8))
+
+        eps = const.tile([P, 1], F32)
+        nc.vector.memset(eps[:], EPS)
+        warm = const.tile([P, 1], F32)
+        nc.scalar.activation(out=warm[:], in_=eps[:], func=ACT.Sqrt)
+        ident = const.tile([P, P], F32)
+        make_identity(nc, ident[:])
+
+        fn_bc = const.tile([P, D], BF16)
+        bias_bc = const.tile([P, D], BF16)
+        kn_bc = const.tile([P, D], BF16)
+        fn_loaded = const.tile([1, D], BF16)
+        nc.sync.dma_start(out=fn_loaded[:], in_=fn_w.unsqueeze(0))
+        fn_row = const.tile([P, D], BF16)
+        nc.vector.memset(fn_row[:].bitcast(I32), 0)
+        nc.vector.tensor_copy(out=fn_row[0:1, :], in_=fn_loaded[:])
+        ones = const.tile([P, P], BF16)
+        nc.vector.memset(ones[:], 1.0)
+
+        def spread_fn_w():
+            for j in range(CHUNKS):
+                cols = slice(j * CHUNK, (j + 1) * CHUNK)
+                bank = psum.tile([P, CHUNK], F32, tag="bank")
+                nc.tensor.matmul(out=bank[:], lhsT=ones[:], rhs=fn_row[:, cols], start=True, stop=True)
+                nc.vector.tensor_copy(out=fn_bc[:, cols], in_=bank[:])
+
+        x_codes = keep.tile([P, TOKEN_TILES, PASSES * P], U32, align_bytes=64)
+        x_scales = keep.tile([P, TOKEN_TILES, PASSES * P], U8, align_bytes=64)
+        w_codes = keep.tile([P, CHUNKS, PASSES * CHUNK], U32, align_bytes=64)
+        w_scales = keep.tile([P, CHUNKS, PASSES * CHUNK], U8, align_bytes=64)
+        x_sumsq = keep.tile([P, TOKEN_TILES], F32)
+        x_rms = keep.tile([P, TOKEN_TILES], F32)
+        x_rstd = keep.tile([P, TOKEN_TILES], F32)
+        k_sumsq_parts = keep.tile([P, TOKEN_TILES, CHUNKS], F32)
+        k_sumsq = keep.tile([P, TOKEN_TILES], F32)
+        k_rms = keep.tile([P, TOKEN_TILES], F32)
+        k_rstd = keep.tile([P, TOKEN_TILES], F32)
+        x_raw = {}
+        k_tiles = {}
+
+        def load_tokens(i):
+            x_raw[i] = x_in.tile([P, D], BF16, name="x_raw")
+            nc.sync.dma_start(out=x_raw[i][:], in_=x_rows[i * P : (i + 1) * P, :])
+
+        def k_onto_partitions(rows_words, grouped_words, copy):
+            for half in range(2):
+                bank = psum.tile([P, 2, 2, P], F32, tag="bank")
+                for c2 in range(2):
+                    for u in range(2):
+                        first = (2 * half + c2) * 2 * P + u
+                        nc.tensor.transpose(bank[:, c2, u, :], rows_words[:, first : first + 2 * P - 1 : 2], ident[:])
+                copy(
+                    out=grouped_words[:, 2 * half : 2 * half + 2, :, :],
+                    in_=bank[:].rearrange("p c u r -> p c r u"),
+                )
+
+        def prepare_tokens(i):
+            squares = work.tile([P, D], BF16)
+            nc.scalar.activation(
+                out=squares[:], in_=x_raw[i][:], func=ACT.Square, accum_out=x_sumsq[:, i : i + 1]
+            )
+            nc.scalar.activation(
+                out=x_rms[:, i : i + 1], in_=x_sumsq[:, i : i + 1], func=ACT.Sqrt, scale=1.0 / D, bias=eps[:]
+            )
+            nc.vector.reciprocal(out=x_rstd[:, i : i + 1], in_=x_rms[:, i : i + 1])
+            x_n = work.tile([P, D], BF16)
+            nc.vector.scalar_tensor_tensor(
+                out=x_n[:], in0=x_raw[i][:], scalar=x_rstd[:, i : i + 1], in1=fn_bc[:], op0=ALU.mult, op1=ALU.mult
+            )
+            x_grouped = work.tile([P, D], BF16, align_bytes=64)
+            k_onto_partitions(
+                x_n[:].bitcast(F32),
+                x_grouped[:].bitcast(F32).rearrange("p (c r u) -> p c r u", c=PASSES, r=P, u=2),
+                nc.vector.tensor_copy if i < EARLY else nc.scalar.copy,
+            )
+            nc.vector.quantize_mx(out=x_codes[:, i, :].bitcast(FP8X4), scales=x_scales[:, i, :], in_=x_grouped[:])
+
+        def prepare_chunk(j):
+            w_grouped = work.tile([P, PASSES * CHUNK * PACK], BF16, align_bytes=64)
+            grouped_words = w_grouped[:].bitcast(F32).rearrange(
+                "p (c n r u) -> p c n r u", c=PASSES, n=W_TILES_PER_CHUNK, r=P, u=2
+            )
+            for n in range(W_TILES_PER_CHUNK):
+                first_row = j * CHUNK + n * P
+                w_raw = w_in.tile([P, D], BF16)
+                nc.sync.dma_start(out=w_raw[:], in_=Wk_w[first_row : first_row + P, :])
+                k_onto_partitions(w_raw[:].bitcast(F32), grouped_words[:, :, n, :, :], nc.scalar.copy)
+            for c in range(PASSES):
+                nc.vector.quantize_mx(
+                    out=w_codes[:, j, c * CHUNK : (c + 1) * CHUNK].bitcast(FP8X4),
+                    scales=w_scales[:, j, c * CHUNK : (c + 1) * CHUNK],
+                    in_=w_grouped[:, c * CHUNK * PACK : (c + 1) * CHUNK * PACK],
+                )
+
+        def multiply(i, j):
+            if i not in k_tiles:
+                k_tiles[i] = k_pool.tile([P, D], F32, name="k_tile")
+            acc = psum.tile([P, CHUNK], F32, tag="bank")
+            for c in range(PASSES):
+                nc.tensor.matmul_mx(
+                    out=acc[:],
+                    lhsT=x_codes[:, i, c * P : (c + 1) * P].bitcast(FP8X4),
+                    lhsT_scale=x_scales[:, i, c * P : (c + 1) * P],
+                    rhs=w_codes[:, j, c * CHUNK : (c + 1) * CHUNK].bitcast(FP8X4),
+                    rhs_scale=w_scales[:, j, c * CHUNK : (c + 1) * CHUNK],
+                    start=(c == 0),
+                    stop=(c == PASSES - 1),
+                )
+            cols = slice(j * CHUNK, (j + 1) * CHUNK)
+            nc.vector.tensor_tensor(out=k_tiles[i][:, cols], in0=acc[:], in1=bias_bc[:, cols], op=ALU.add)
+
+        def finish(i):
+            k_tile = k_tiles[i]
+            for j in range(CHUNKS):
+                k_squares = work.tile([P, CHUNK], BF16)
+                nc.scalar.activation(
+                    out=k_squares[:],
+                    in_=k_tile[:, j * CHUNK : (j + 1) * CHUNK],
+                    func=ACT.Square,
+                    accum_out=k_sumsq_parts[:, i, j : j + 1],
+                )
+            parts_copy = work.tile([P, CHUNKS], F32)
+            nc.scalar.activation(
+                out=parts_copy[:], in_=k_sumsq_parts[:, i, :], func=ACT.Identity, accum_out=k_sumsq[:, i : i + 1]
+            )
+            nc.scalar.activation(
+                out=k_rms[:, i : i + 1], in_=k_sumsq[:, i : i + 1], func=ACT.Sqrt, scale=1.0 / D, bias=eps[:]
+            )
+            nc.vector.reciprocal(out=k_rstd[:, i : i + 1], in_=k_rms[:, i : i + 1])
+            nc.vector.scalar_tensor_tensor(
+                out=k_tile[:], in0=k_tile[:], scalar=k_rstd[:, i : i + 1], in1=kn_bc[:], op0=ALU.mult, op1=ALU.mult
+            )
+            nc.sync.dma_start(out=out_rows[i * P : (i + 1) * P, :], in_=k_tile[:])
+
+        def prepare_round(r):
+            load_tokens(r)
+            prepare_tokens(r)
+            if r < CHUNKS:
+                prepare_chunk(r)
+
+        spread_fn_w()
+        prepare_round(0)
+        nc.sync.dma_start(out=bias_bc[:], in_=Wk_b.partition_broadcast(P))
+        for r in range(TOKEN_TILES):
+            if r + 1 < TOKEN_TILES:
+                prepare_round(r + 1)
+            if r == CHUNKS:
+                nc.sync.dma_start(out=kn_bc[:], in_=kn_w.partition_broadcast(P))
+            if r < CHUNKS:
+                for j in range(r):
+                    multiply(r, j)
+                for i in range(r + 1):
+                    multiply(i, r)
+            else:
+                for j in range(CHUNKS):
+                    multiply(r, j)
+                finish(r - CHUNKS)
+        for i in range(TOKEN_TILES - CHUNKS, TOKEN_TILES):
+            finish(i)

@@ -19,12 +19,15 @@ EPS = 1e-6
 PACK = 4
 K_PASS = P * PACK
 PASSES = D // K_PASS
-WORDS = D // 2
 CHUNK = 512
 CHUNKS = D // CHUNK
 W_TILES_PER_CHUNK = CHUNK // P
 TOKEN_TILES = TOKENS // P
-EARLY = 4
+EARLY_PRODUCTS = {
+    1: (((0, 0),), ()),
+    2: (((0, 1), (1, 0)), ((1, 1),)),
+    3: (((0, 2), (1, 2)), ((2, 0), (2, 1), (2, 2))),
+}
 
 FLOPS = 2 * TOKENS * D * D
 
@@ -40,13 +43,15 @@ def tile_crossattention_pa_kernel(tc, features, fn_w, Wk_w, Wk_b, kn_w, out):
         x_in = ctx.enter_context(tc.tile_pool(name="x_in", bufs=4))
         w_in = ctx.enter_context(tc.tile_pool(name="w_in", bufs=6))
         work = ctx.enter_context(tc.tile_pool(name="work", bufs=2))
-        k_pool = ctx.enter_context(tc.tile_pool(name="k_pool", bufs=EARLY + 2))
+        stats = ctx.enter_context(tc.tile_pool(name="stats", bufs=2 * TOKEN_TILES))
+        junk_pool = ctx.enter_context(tc.tile_pool(name="junk_pool", bufs=1))
+        k_pool = ctx.enter_context(tc.tile_pool(name="k_pool", bufs=6))
         psum = ctx.enter_context(tc.psum_pool(name="psum", bufs=8))
 
-        eps = const.tile([P, 1], F32)
-        nc.vector.memset(eps[:], EPS)
+        neg_half = const.tile([P, 1], F32)
+        nc.gpsimd.memset(neg_half[:], -0.5)
         warm = const.tile([P, 1], F32)
-        nc.scalar.activation(out=warm[:], in_=eps[:], func=ACT.Sqrt)
+        nc.scalar.activation(out=warm[:], in_=neg_half[:], func=ACT.Square)
         ident = const.tile([P, P], F32)
         make_identity(nc, ident[:])
 
@@ -66,74 +71,104 @@ def tile_crossattention_pa_kernel(tc, features, fn_w, Wk_w, Wk_b, kn_w, out):
                 cols = slice(j * CHUNK, (j + 1) * CHUNK)
                 bank = psum.tile([P, CHUNK], F32, tag="bank")
                 nc.tensor.matmul(out=bank[:], lhsT=ones[:], rhs=fn_row[:, cols], start=True, stop=True)
-                nc.vector.tensor_copy(out=fn_bc[:, cols], in_=bank[:])
+                copy = nc.vector.tensor_copy if j % 2 == 0 else nc.scalar.copy
+                copy(out=fn_bc[:, cols], in_=bank[:])
 
         x_codes = keep.tile([P, TOKEN_TILES, PASSES * P], U32, align_bytes=64)
         x_scales = keep.tile([P, TOKEN_TILES, PASSES * P], U8, align_bytes=64)
         w_codes = keep.tile([P, CHUNKS, PASSES * CHUNK], U32, align_bytes=64)
         w_scales = keep.tile([P, CHUNKS, PASSES * CHUNK], U8, align_bytes=64)
-        x_sumsq = keep.tile([P, TOKEN_TILES], F32)
-        x_rms = keep.tile([P, TOKEN_TILES], F32)
-        x_rstd = keep.tile([P, TOKEN_TILES], F32)
-        k_sumsq_parts = keep.tile([P, TOKEN_TILES, CHUNKS], F32)
-        k_sumsq = keep.tile([P, TOKEN_TILES], F32)
-        k_rms = keep.tile([P, TOKEN_TILES], F32)
-        k_rstd = keep.tile([P, TOKEN_TILES], F32)
         x_raw = {}
+        x_rstd = {}
+        x_n = {}
+        x_banks = {}
+        x_grouped = {}
+        w_grouped = {}
+        k_rstd = {}
+        w_raw = {}
         k_tiles = {}
 
         def load_tokens(i):
             x_raw[i] = x_in.tile([P, D], BF16, name="x_raw")
             nc.sync.dma_start(out=x_raw[i][:], in_=x_rows[i * P : (i + 1) * P, :])
 
-        def k_onto_partitions(rows_words, grouped_words, copy):
+        def load_weights(n):
+            w_raw[n] = w_in.tile([P, D], BF16, name="w_raw")
+            nc.sync.dma_start(out=w_raw[n][:], in_=Wk_w[n * P : (n + 1) * P, :])
+
+        def inverse_rms(values):
+            junk = junk_pool.tile([P, D], BF16, name="junk")
+            sumsq = stats.tile([P, 1], F32, name="sumsq")
+            nc.scalar.activation(out=junk[:], in_=values, func=ACT.Square, accum_out=sumsq[:])
+            meansq = stats.tile([P, 1], F32, name="meansq")
+            nc.gpsimd.tensor_scalar(
+                out=meansq[:], in0=sumsq[:], scalar1=1.0 / D, scalar2=EPS, op0=ALU.mult, op1=ALU.add
+            )
+            rstd = stats.tile([P, 1], F32, name="rstd")
+            nc.gpsimd.tensor_tensor(out=rstd[:], in0=meansq[:], in1=neg_half[:], op=ALU.pow)
+            return rstd
+
+        def transpose_words(words_of):
+            banks = []
             for half in range(2):
-                bank = psum.tile([P, 2, 2, P], F32, tag="bank")
+                bank = psum.tile([P, 2, 2, P], F32, tag="bank", name="bank")
                 for c2 in range(2):
                     for u in range(2):
-                        first = (2 * half + c2) * 2 * P + u
-                        nc.tensor.transpose(bank[:, c2, u, :], rows_words[:, first : first + 2 * P - 1 : 2], ident[:])
-                copy(
-                    out=grouped_words[:, 2 * half : 2 * half + 2, :, :],
-                    in_=bank[:].rearrange("p c u r -> p c r u"),
+                        nc.tensor.transpose(bank[:, c2, u, :], words_of(2 * half + c2, u), ident[:])
+                banks.append(bank)
+            return banks
+
+        def interleave(banks, copies, grouped_of):
+            for half in range(2):
+                copies[half](out=grouped_of(half), in_=banks[half][:].rearrange("p c u r -> p c r u"))
+
+        def scale_tokens(i):
+            x_n[i] = work.tile([P, 2, D // 2], BF16, name="x_n")
+            x_pairs = x_raw[i][:].rearrange("p (w u e) -> p u w e", u=2, e=2)
+            fn_pairs = fn_bc[:].rearrange("p (w u e) -> p u w e", u=2, e=2)
+            for u in range(2):
+                nc.vector.scalar_tensor_tensor(
+                    out=x_n[i][:, u, :].rearrange("p (w e) -> p w e", e=2),
+                    in0=x_pairs[:, u],
+                    scalar=x_rstd[i][:],
+                    in1=fn_pairs[:, u],
+                    op0=ALU.mult,
+                    op1=ALU.mult,
                 )
 
-        def prepare_tokens(i):
-            squares = work.tile([P, D], BF16)
-            nc.scalar.activation(
-                out=squares[:], in_=x_raw[i][:], func=ACT.Square, accum_out=x_sumsq[:, i : i + 1]
-            )
-            nc.scalar.activation(
-                out=x_rms[:, i : i + 1], in_=x_sumsq[:, i : i + 1], func=ACT.Sqrt, scale=1.0 / D, bias=eps[:]
-            )
-            nc.vector.reciprocal(out=x_rstd[:, i : i + 1], in_=x_rms[:, i : i + 1])
-            x_n = work.tile([P, D], BF16)
-            nc.vector.scalar_tensor_tensor(
-                out=x_n[:], in0=x_raw[i][:], scalar=x_rstd[:, i : i + 1], in1=fn_bc[:], op0=ALU.mult, op1=ALU.mult
-            )
-            x_grouped = work.tile([P, D], BF16, align_bytes=64)
-            k_onto_partitions(
-                x_n[:].bitcast(F32),
-                x_grouped[:].bitcast(F32).rearrange("p (c r u) -> p c r u", c=PASSES, r=P, u=2),
-                nc.vector.tensor_copy if i < EARLY else nc.scalar.copy,
-            )
-            nc.vector.quantize_mx(out=x_codes[:, i, :].bitcast(FP8X4), scales=x_scales[:, i, :], in_=x_grouped[:])
+        def transpose_tokens(i):
+            words = x_n[i][:].rearrange("p u w -> p (u w)").bitcast(F32)
+            x_banks[i] = transpose_words(lambda c, u: words[:, (u * PASSES + c) * P : (u * PASSES + c + 1) * P])
 
-        def prepare_chunk(j):
-            w_grouped = work.tile([P, PASSES * CHUNK * PACK], BF16, align_bytes=64)
-            grouped_words = w_grouped[:].bitcast(F32).rearrange(
+        def interleave_tokens(i):
+            x_grouped[i] = work.tile([P, D], BF16, name="x_grouped", align_bytes=64)
+            grouped = x_grouped[i][:].bitcast(F32).rearrange("p (c r u) -> p c r u", c=PASSES, r=P, u=2)
+            interleave(x_banks[i], (nc.scalar.copy, nc.scalar.copy), lambda half: grouped[:, 2 * half : 2 * half + 2])
+
+        def quantise_tokens(i):
+            nc.vector.quantize_mx(out=x_codes[:, i, :].bitcast(FP8X4), scales=x_scales[:, i, :], in_=x_grouped[i][:])
+
+        def transpose_weights(n):
+            j, m = divmod(n, W_TILES_PER_CHUNK)
+            if m == 0:
+                w_grouped[j] = work.tile([P, PASSES * CHUNK * PACK], BF16, name="w_grouped", align_bytes=64)
+            grouped = w_grouped[j][:].bitcast(F32).rearrange(
                 "p (c n r u) -> p c n r u", c=PASSES, n=W_TILES_PER_CHUNK, r=P, u=2
             )
-            for n in range(W_TILES_PER_CHUNK):
-                first_row = j * CHUNK + n * P
-                w_raw = w_in.tile([P, D], BF16)
-                nc.sync.dma_start(out=w_raw[:], in_=Wk_w[first_row : first_row + P, :])
-                k_onto_partitions(w_raw[:].bitcast(F32), grouped_words[:, :, n, :, :], nc.scalar.copy)
-            for c in range(PASSES):
+            words = w_raw[n][:].bitcast(F32)
+            banks = transpose_words(lambda c, u: words[:, 2 * P * c + u : 2 * P * (c + 1) : 2])
+            copies = [nc.scalar.copy, nc.scalar.copy]
+            if j == 0:
+                copies[(n + 1) % 2] = nc.vector.tensor_copy
+            interleave(banks, copies, lambda half: grouped[:, 2 * half : 2 * half + 2, m])
+
+        def quantise_weights(j):
+            for half in range(2):
+                cols = slice(half * 2 * CHUNK, (half + 1) * 2 * CHUNK)
                 nc.vector.quantize_mx(
-                    out=w_codes[:, j, c * CHUNK : (c + 1) * CHUNK].bitcast(FP8X4),
-                    scales=w_scales[:, j, c * CHUNK : (c + 1) * CHUNK],
-                    in_=w_grouped[:, c * CHUNK * PACK : (c + 1) * CHUNK * PACK],
+                    out=w_codes[:, j, cols].bitcast(FP8X4),
+                    scales=w_scales[:, j, cols],
+                    in_=w_grouped[j][:, half * 2 * CHUNK * PACK : (half + 1) * 2 * CHUNK * PACK],
                 )
 
         def multiply(i, j):
@@ -155,49 +190,82 @@ def tile_crossattention_pa_kernel(tc, features, fn_w, Wk_w, Wk_b, kn_w, out):
 
         def finish(i):
             k_tile = k_tiles[i]
-            for j in range(CHUNKS):
-                k_squares = work.tile([P, CHUNK], BF16)
-                nc.scalar.activation(
-                    out=k_squares[:],
-                    in_=k_tile[:, j * CHUNK : (j + 1) * CHUNK],
-                    func=ACT.Square,
-                    accum_out=k_sumsq_parts[:, i, j : j + 1],
+            for half in range(2):
+                cols = slice(half * D // 2, (half + 1) * D // 2)
+                nc.vector.scalar_tensor_tensor(
+                    out=k_tile[:, cols],
+                    in0=k_tile[:, cols],
+                    scalar=k_rstd[i][:],
+                    in1=kn_bc[:, cols],
+                    op0=ALU.mult,
+                    op1=ALU.mult,
                 )
-            parts_copy = work.tile([P, CHUNKS], F32)
-            nc.scalar.activation(
-                out=parts_copy[:], in_=k_sumsq_parts[:, i, :], func=ACT.Identity, accum_out=k_sumsq[:, i : i + 1]
-            )
-            nc.scalar.activation(
-                out=k_rms[:, i : i + 1], in_=k_sumsq[:, i : i + 1], func=ACT.Sqrt, scale=1.0 / D, bias=eps[:]
-            )
-            nc.vector.reciprocal(out=k_rstd[:, i : i + 1], in_=k_rms[:, i : i + 1])
-            nc.vector.scalar_tensor_tensor(
-                out=k_tile[:], in0=k_tile[:], scalar=k_rstd[:, i : i + 1], in1=kn_bc[:], op0=ALU.mult, op1=ALU.mult
-            )
-            nc.sync.dma_start(out=out_rows[i * P : (i + 1) * P, :], in_=k_tile[:])
+                nc.sync.dma_start(out=out_rows[i * P : (i + 1) * P, cols], in_=k_tile[:, cols])
 
-        def prepare_round(r):
-            load_tokens(r)
-            prepare_tokens(r)
-            if r < CHUNKS:
-                prepare_chunk(r)
+        def load_chunk(j):
+            for n in range(j * W_TILES_PER_CHUNK, (j + 1) * W_TILES_PER_CHUNK):
+                load_weights(n)
 
+        def square_tokens(i):
+            x_rstd[i] = inverse_rms(x_raw[i][:])
+
+        ctx.enter_context(tc.manual_schedule())
         spread_fn_w()
-        prepare_round(0)
+        load_tokens(0)
+        load_chunk(0)
+        load_tokens(1)
         nc.sync.dma_start(out=bias_bc[:], in_=Wk_b.partition_broadcast(P))
-        for r in range(TOKEN_TILES):
-            if r + 1 < TOKEN_TILES:
-                prepare_round(r + 1)
-            if r == CHUNKS:
-                nc.sync.dma_start(out=kn_bc[:], in_=kn_w.partition_broadcast(P))
-            if r < CHUNKS:
-                for j in range(r):
-                    multiply(r, j)
-                for i in range(r + 1):
-                    multiply(i, r)
-            else:
-                for j in range(CHUNKS):
-                    multiply(r, j)
-                finish(r - CHUNKS)
-        for i in range(TOKEN_TILES - CHUNKS, TOKEN_TILES):
-            finish(i)
+        load_chunk(1)
+        square_tokens(0)
+        transpose_weights(0)
+        transpose_weights(1)
+        scale_tokens(0)
+        transpose_weights(2)
+        transpose_weights(3)
+        transpose_tokens(0)
+        quantise_weights(0)
+        square_tokens(1)
+        interleave_tokens(0)
+        quantise_tokens(0)
+        scale_tokens(1)
+        for r in range(1, CHUNKS):
+            load_tokens(r + 1)
+            if r + 1 < CHUNKS:
+                load_chunk(r + 1)
+            first = r * W_TILES_PER_CHUNK
+            for n in range(first, first + 3):
+                transpose_weights(n)
+            for i, j in EARLY_PRODUCTS[r][0]:
+                multiply(i, j)
+            transpose_weights(first + 3)
+            transpose_tokens(r)
+            quantise_weights(r)
+            interleave_tokens(r)
+            square_tokens(r + 1)
+            quantise_tokens(r)
+            for i, j in EARLY_PRODUCTS[r][1]:
+                multiply(i, j)
+            scale_tokens(r + 1)
+        load_tokens(CHUNKS + 1)
+        nc.sync.dma_start(out=kn_bc[:], in_=kn_w.partition_broadcast(P))
+        early = [product for run in EARLY_PRODUCTS.values() for part in run for product in part]
+        for s in range(TOKEN_TILES):
+            ahead = s + CHUNKS
+            if ahead + 2 < TOKEN_TILES:
+                load_tokens(ahead + 2)
+            if ahead + 1 < TOKEN_TILES:
+                square_tokens(ahead + 1)
+            for j in range(CHUNKS):
+                if (s, j) not in early:
+                    multiply(s, j)
+            if ahead < TOKEN_TILES:
+                transpose_tokens(ahead)
+                interleave_tokens(ahead)
+            if s > 0:
+                finish(s - 1)
+            if ahead + 1 < TOKEN_TILES:
+                scale_tokens(ahead + 1)
+            if ahead < TOKEN_TILES:
+                quantise_tokens(ahead)
+            k_rstd[s] = inverse_rms(k_tiles[s][:])
+        finish(TOKEN_TILES - 1)

@@ -48,10 +48,10 @@ def tile_crossattention_pa_kernel(tc, features, fn_w, Wk_w, Wk_b, kn_w, out):
         k_pool = ctx.enter_context(tc.tile_pool(name="k_pool", bufs=6))
         psum = ctx.enter_context(tc.psum_pool(name="psum", bufs=8))
 
-        neg_half = const.tile([P, 1], F32)
-        nc.gpsimd.memset(neg_half[:], -0.5)
+        eps = const.tile([P, 1], F32)
+        nc.vector.memset(eps[:], EPS)
         warm = const.tile([P, 1], F32)
-        nc.scalar.activation(out=warm[:], in_=neg_half[:], func=ACT.Square)
+        nc.scalar.activation(out=warm[:], in_=eps[:], func=ACT.Sqrt)
         ident = const.tile([P, P], F32)
         make_identity(nc, ident[:])
 
@@ -71,19 +71,20 @@ def tile_crossattention_pa_kernel(tc, features, fn_w, Wk_w, Wk_b, kn_w, out):
                 cols = slice(j * CHUNK, (j + 1) * CHUNK)
                 bank = psum.tile([P, CHUNK], F32, tag="bank")
                 nc.tensor.matmul(out=bank[:], lhsT=ones[:], rhs=fn_row[:, cols], start=True, stop=True)
-                copy = nc.vector.tensor_copy if j % 2 == 0 else nc.scalar.copy
-                copy(out=fn_bc[:, cols], in_=bank[:])
+                nc.vector.tensor_copy(out=fn_bc[:, cols], in_=bank[:])
 
         x_codes = keep.tile([P, TOKEN_TILES, PASSES * P], U32, align_bytes=64)
         x_scales = keep.tile([P, TOKEN_TILES, PASSES * P], U8, align_bytes=64)
         w_codes = keep.tile([P, CHUNKS, PASSES * CHUNK], U32, align_bytes=64)
         w_scales = keep.tile([P, CHUNKS, PASSES * CHUNK], U8, align_bytes=64)
         x_raw = {}
+        x_rms = {}
         x_rstd = {}
         x_n = {}
         x_banks = {}
         x_grouped = {}
         w_grouped = {}
+        k_rms = {}
         k_rstd = {}
         w_raw = {}
         k_tiles = {}
@@ -96,16 +97,17 @@ def tile_crossattention_pa_kernel(tc, features, fn_w, Wk_w, Wk_b, kn_w, out):
             w_raw[n] = w_in.tile([P, D], BF16, name="w_raw")
             nc.sync.dma_start(out=w_raw[n][:], in_=Wk_w[n * P : (n + 1) * P, :])
 
-        def inverse_rms(values):
+        def root_mean_square(values):
             junk = junk_pool.tile([P, D], BF16, name="junk")
             sumsq = stats.tile([P, 1], F32, name="sumsq")
             nc.scalar.activation(out=junk[:], in_=values, func=ACT.Square, accum_out=sumsq[:])
-            meansq = stats.tile([P, 1], F32, name="meansq")
-            nc.gpsimd.tensor_scalar(
-                out=meansq[:], in0=sumsq[:], scalar1=1.0 / D, scalar2=EPS, op0=ALU.mult, op1=ALU.add
-            )
+            rms = stats.tile([P, 1], F32, name="rms")
+            nc.scalar.activation(out=rms[:], in_=sumsq[:], func=ACT.Sqrt, scale=1.0 / D, bias=eps[:])
+            return rms
+
+        def invert(rms):
             rstd = stats.tile([P, 1], F32, name="rstd")
-            nc.gpsimd.tensor_tensor(out=rstd[:], in0=meansq[:], in1=neg_half[:], op=ALU.pow)
+            nc.vector.reciprocal(out=rstd[:], in_=rms[:])
             return rstd
 
         def transpose_words(words_of):
@@ -207,18 +209,19 @@ def tile_crossattention_pa_kernel(tc, features, fn_w, Wk_w, Wk_b, kn_w, out):
                 load_weights(n)
 
         def square_tokens(i):
-            x_rstd[i] = inverse_rms(x_raw[i][:])
+            x_rms[i] = root_mean_square(x_raw[i][:])
 
         ctx.enter_context(tc.manual_schedule())
         spread_fn_w()
         load_tokens(0)
         load_chunk(0)
         load_tokens(1)
-        nc.sync.dma_start(out=bias_bc[:], in_=Wk_b.partition_broadcast(P))
         load_chunk(1)
+        nc.sync.dma_start(out=bias_bc[:], in_=Wk_b.partition_broadcast(P))
         square_tokens(0)
         transpose_weights(0)
         transpose_weights(1)
+        x_rstd[0] = invert(x_rms[0])
         scale_tokens(0)
         transpose_weights(2)
         transpose_weights(3)
@@ -227,6 +230,7 @@ def tile_crossattention_pa_kernel(tc, features, fn_w, Wk_w, Wk_b, kn_w, out):
         square_tokens(1)
         interleave_tokens(0)
         quantise_tokens(0)
+        x_rstd[1] = invert(x_rms[1])
         scale_tokens(1)
         for r in range(1, CHUNKS):
             load_tokens(r + 1)
@@ -243,7 +247,10 @@ def tile_crossattention_pa_kernel(tc, features, fn_w, Wk_w, Wk_b, kn_w, out):
             interleave_tokens(r)
             square_tokens(r + 1)
             quantise_tokens(r)
-            for i, j in EARLY_PRODUCTS[r][1]:
+            for i, j in EARLY_PRODUCTS[r][1][:-1]:
+                multiply(i, j)
+            x_rstd[r + 1] = invert(x_rms[r + 1])
+            for i, j in EARLY_PRODUCTS[r][1][-1:]:
                 multiply(i, j)
             scale_tokens(r + 1)
         load_tokens(CHUNKS + 1)
@@ -256,6 +263,11 @@ def tile_crossattention_pa_kernel(tc, features, fn_w, Wk_w, Wk_b, kn_w, out):
             if ahead + 1 < TOKEN_TILES:
                 square_tokens(ahead + 1)
             for j in range(CHUNKS):
+                if j == CHUNKS - 1:
+                    if s > 0:
+                        k_rstd[s - 1] = invert(k_rms[s - 1])
+                    if ahead + 1 < TOKEN_TILES:
+                        x_rstd[ahead + 1] = invert(x_rms[ahead + 1])
                 if (s, j) not in early:
                     multiply(s, j)
             if ahead < TOKEN_TILES:
@@ -267,5 +279,6 @@ def tile_crossattention_pa_kernel(tc, features, fn_w, Wk_w, Wk_b, kn_w, out):
                 scale_tokens(ahead + 1)
             if ahead < TOKEN_TILES:
                 quantise_tokens(ahead)
-            k_rstd[s] = inverse_rms(k_tiles[s][:])
+            k_rms[s] = root_mean_square(k_tiles[s][:])
+        k_rstd[TOKEN_TILES - 1] = invert(k_rms[TOKEN_TILES - 1])
         finish(TOKEN_TILES - 1)

@@ -24,9 +24,8 @@ CHUNKS = D // CHUNK
 W_TILES_PER_CHUNK = CHUNK // P
 TOKEN_TILES = TOKENS // P
 EARLY_PRODUCTS = {
-    1: (((0, 0),), ()),
-    2: (((0, 1), (1, 0)), ((1, 1),)),
-    3: (((0, 2), (1, 2)), ((2, 0), (2, 1), (2, 2))),
+    2: ((0, 0), (1, 0)),
+    3: ((0, 1), (1, 1), (2, 0), (2, 1), (0, 2)),
 }
 
 FLOPS = 2 * TOKENS * D * D
@@ -161,7 +160,7 @@ def tile_crossattention_pa_kernel(tc, features, fn_w, Wk_w, Wk_b, kn_w, out):
             banks = transpose_words(lambda c, u: words[:, 2 * P * c + u : 2 * P * (c + 1) : 2])
             copies = [nc.scalar.copy, nc.scalar.copy]
             if j == 0:
-                copies[(n + 1) % 2] = nc.vector.tensor_copy
+                copies[n % 2] = nc.vector.tensor_copy
             interleave(banks, copies, lambda half: grouped[:, 2 * half : 2 * half + 2, m])
 
         def quantise_weights(j):
@@ -211,65 +210,67 @@ def tile_crossattention_pa_kernel(tc, features, fn_w, Wk_w, Wk_b, kn_w, out):
         def square_tokens(i):
             x_rms[i] = root_mean_square(x_raw[i][:])
 
+        def scale_tokens_by_rms(i):
+            x_rstd[i] = invert(x_rms[i])
+            scale_tokens(i)
+
         ctx.enter_context(tc.manual_schedule())
         spread_fn_w()
         load_tokens(0)
         load_chunk(0)
         load_tokens(1)
         load_chunk(1)
-        nc.sync.dma_start(out=bias_bc[:], in_=Wk_b.partition_broadcast(P))
+        load_tokens(2)
         square_tokens(0)
         transpose_weights(0)
         transpose_weights(1)
         x_rstd[0] = invert(x_rms[0])
-        scale_tokens(0)
         transpose_weights(2)
-        transpose_weights(3)
-        transpose_tokens(0)
-        quantise_weights(0)
         square_tokens(1)
-        interleave_tokens(0)
-        quantise_tokens(0)
-        x_rstd[1] = invert(x_rms[1])
-        scale_tokens(1)
+        transpose_weights(3)
+        scale_tokens(0)
+        quantise_weights(0)
         for r in range(1, CHUNKS):
-            load_tokens(r + 1)
             if r + 1 < CHUNKS:
                 load_chunk(r + 1)
+                if r == 1:
+                    nc.sync.dma_start(out=bias_bc[:], in_=Wk_b.partition_broadcast(P))
+            load_tokens(r + 2)
             first = r * W_TILES_PER_CHUNK
-            for n in range(first, first + 3):
-                transpose_weights(n)
-            for i, j in EARLY_PRODUCTS[r][0]:
-                multiply(i, j)
-            transpose_weights(first + 3)
-            transpose_tokens(r)
-            quantise_weights(r)
-            interleave_tokens(r)
+            transpose_weights(first)
+            transpose_weights(first + 1)
+            transpose_tokens(r - 1)
+            interleave_tokens(r - 1)
+            scale_tokens_by_rms(r)
+            quantise_tokens(r - 1)
+            transpose_weights(first + 2)
             square_tokens(r + 1)
-            quantise_tokens(r)
-            for i, j in EARLY_PRODUCTS[r][1][:-1]:
+            transpose_weights(first + 3)
+            quantise_weights(r)
+            for i, j in EARLY_PRODUCTS.get(r, ()):
                 multiply(i, j)
-            x_rstd[r + 1] = invert(x_rms[r + 1])
-            for i, j in EARLY_PRODUCTS[r][1][-1:]:
-                multiply(i, j)
-            scale_tokens(r + 1)
-        load_tokens(CHUNKS + 1)
+        load_tokens(CHUNKS + 2)
         nc.sync.dma_start(out=kn_bc[:], in_=kn_w.partition_broadcast(P))
-        early = [product for run in EARLY_PRODUCTS.values() for part in run for product in part]
+        transpose_tokens(CHUNKS - 1)
+        interleave_tokens(CHUNKS - 1)
+        scale_tokens_by_rms(CHUNKS)
+        quantise_tokens(CHUNKS - 1)
+        square_tokens(CHUNKS + 1)
+        early = [product for run in EARLY_PRODUCTS.values() for product in run]
         for s in range(TOKEN_TILES):
             ahead = s + CHUNKS
+            if ahead + 3 < TOKEN_TILES:
+                load_tokens(ahead + 3)
             if ahead + 2 < TOKEN_TILES:
-                load_tokens(ahead + 2)
-            if ahead + 1 < TOKEN_TILES:
-                square_tokens(ahead + 1)
-            for j in range(CHUNKS):
-                if j == CHUNKS - 1:
+                square_tokens(ahead + 2)
+            left = [j for j in range(CHUNKS) if (s, j) not in early]
+            for j in left:
+                if j == left[-1]:
                     if s > 0:
                         k_rstd[s - 1] = invert(k_rms[s - 1])
                     if ahead + 1 < TOKEN_TILES:
                         x_rstd[ahead + 1] = invert(x_rms[ahead + 1])
-                if (s, j) not in early:
-                    multiply(s, j)
+                multiply(s, j)
             if ahead < TOKEN_TILES:
                 transpose_tokens(ahead)
                 interleave_tokens(ahead)

@@ -23,10 +23,8 @@ CHUNK = 512
 CHUNKS = D // CHUNK
 W_TILES_PER_CHUNK = CHUNK // P
 TOKEN_TILES = TOKENS // P
-EARLY_PRODUCTS = {
-    2: ((0, 0), (1, 0)),
-    3: ((0, 1), (1, 1), (2, 0), (2, 1), (0, 2)),
-}
+W_TILES = D // P
+EARLY = 3
 
 FLOPS = 2 * TOKENS * D * D
 
@@ -39,12 +37,13 @@ def tile_crossattention_pa_kernel(tc, features, fn_w, Wk_w, Wk_b, kn_w, out):
     with ExitStack() as ctx:
         const = ctx.enter_context(tc.tile_pool(name="const", bufs=1))
         keep = ctx.enter_context(tc.tile_pool(name="keep", bufs=1))
-        x_in = ctx.enter_context(tc.tile_pool(name="x_in", bufs=4))
-        w_in = ctx.enter_context(tc.tile_pool(name="w_in", bufs=6))
+        x_in = ctx.enter_context(tc.tile_pool(name="x_in", bufs=6))
+        w_in = ctx.enter_context(tc.tile_pool(name="w_in", bufs=8))
         work = ctx.enter_context(tc.tile_pool(name="work", bufs=2))
         stats = ctx.enter_context(tc.tile_pool(name="stats", bufs=2 * TOKEN_TILES))
         junk_pool = ctx.enter_context(tc.tile_pool(name="junk_pool", bufs=1))
-        k_pool = ctx.enter_context(tc.tile_pool(name="k_pool", bufs=6))
+        gained_pool = ctx.enter_context(tc.tile_pool(name="gained_pool", bufs=3))
+        k_pool = ctx.enter_context(tc.tile_pool(name="k_pool", bufs=4))
         psum = ctx.enter_context(tc.psum_pool(name="psum", bufs=8))
 
         eps = const.tile([P, 1], F32)
@@ -56,12 +55,12 @@ def tile_crossattention_pa_kernel(tc, features, fn_w, Wk_w, Wk_b, kn_w, out):
 
         fn_bc = const.tile([P, D], BF16)
         bias_bc = const.tile([P, D], BF16)
-        kn_bc = const.tile([P, D], BF16)
+        kn_bc = const.tile([P, D // 2], BF16)
         fn_loaded = const.tile([1, D], BF16)
         nc.sync.dma_start(out=fn_loaded[:], in_=fn_w.unsqueeze(0))
-        fn_row = const.tile([P, D], BF16)
-        nc.vector.memset(fn_row[:].bitcast(I32), 0)
-        nc.vector.tensor_copy(out=fn_row[0:1, :], in_=fn_loaded[:])
+        row = const.tile([P, D], BF16)
+        nc.vector.memset(row[:].bitcast(I32), 0)
+        nc.vector.tensor_copy(out=row[0:1, :], in_=fn_loaded[:])
         ones = const.tile([P, P], BF16)
         nc.vector.memset(ones[:], 1.0)
 
@@ -69,13 +68,22 @@ def tile_crossattention_pa_kernel(tc, features, fn_w, Wk_w, Wk_b, kn_w, out):
             for j in range(CHUNKS):
                 cols = slice(j * CHUNK, (j + 1) * CHUNK)
                 bank = psum.tile([P, CHUNK], F32, tag="bank")
-                nc.tensor.matmul(out=bank[:], lhsT=ones[:], rhs=fn_row[:, cols], start=True, stop=True)
+                nc.tensor.matmul(out=bank[:], lhsT=ones[:], rhs=row[:, cols], start=True, stop=True)
                 nc.vector.tensor_copy(out=fn_bc[:, cols], in_=bank[:])
+
+        def spread_kn_w():
+            nc.sync.dma_start(out=row[0:1, :], in_=kn_w.unsqueeze(0))
+            kn_bank = psum.tile([P, D // 2], BF16, tag="bank", name="kn_bank")
+            for part in range(2):
+                cols = slice(part * CHUNK, (part + 1) * CHUNK)
+                nc.tensor.matmul(out=kn_bank[:, cols], lhsT=ones[:], rhs=row[:, cols], start=True, stop=True)
+            return kn_bank
 
         x_codes = keep.tile([P, TOKEN_TILES, PASSES * P], U32, align_bytes=64)
         x_scales = keep.tile([P, TOKEN_TILES, PASSES * P], U8, align_bytes=64)
         w_codes = keep.tile([P, CHUNKS, PASSES * CHUNK], U32, align_bytes=64)
         w_scales = keep.tile([P, CHUNKS, PASSES * CHUNK], U8, align_bytes=64)
+        k_gained = {}
         x_raw = {}
         x_rms = {}
         x_rstd = {}
@@ -161,6 +169,8 @@ def tile_crossattention_pa_kernel(tc, features, fn_w, Wk_w, Wk_b, kn_w, out):
             copies = [nc.scalar.copy, nc.scalar.copy]
             if j == 0:
                 copies[n % 2] = nc.vector.tensor_copy
+            elif n % 2 == 1:
+                copies[1] = nc.vector.tensor_copy
             interleave(banks, copies, lambda half: grouped[:, 2 * half : 2 * half + 2, m])
 
         def quantise_weights(j):
@@ -189,83 +199,63 @@ def tile_crossattention_pa_kernel(tc, features, fn_w, Wk_w, Wk_b, kn_w, out):
             cols = slice(j * CHUNK, (j + 1) * CHUNK)
             nc.vector.tensor_tensor(out=k_tiles[i][:, cols], in0=acc[:], in1=bias_bc[:, cols], op=ALU.add)
 
-        def finish(i):
-            k_tile = k_tiles[i]
-            for half in range(2):
-                cols = slice(half * D // 2, (half + 1) * D // 2)
-                nc.vector.scalar_tensor_tensor(
-                    out=k_tile[:, cols],
-                    in0=k_tile[:, cols],
-                    scalar=k_rstd[i][:],
-                    in1=kn_bc[:, cols],
-                    op0=ALU.mult,
-                    op1=ALU.mult,
-                )
-                nc.sync.dma_start(out=out_rows[i * P : (i + 1) * P, cols], in_=k_tile[:, cols])
+        def gain_second_half(i):
+            k_gained[i] = gained_pool.tile([P, D // 2], F32, name="gained")
+            nc.gpsimd.tensor_tensor(out=k_gained[i][:], in0=k_tiles[i][:, D // 2 :], in1=kn_bc[:], op=ALU.mult)
 
-        def load_chunk(j):
-            for n in range(j * W_TILES_PER_CHUNK, (j + 1) * W_TILES_PER_CHUNK):
-                load_weights(n)
+        def finish(i):
+            first, second = k_tiles[i][:, : D // 2], k_gained[i][:]
+            rows = slice(i * P, (i + 1) * P)
+            nc.scalar.activation(out=second, in_=second, func=ACT.Copy, scale=k_rstd[i][:])
+            nc.vector.scalar_tensor_tensor(
+                out=first, in0=first, scalar=k_rstd[i][:], in1=kn_bank[:], op0=ALU.mult, op1=ALU.mult
+            )
+            nc.sync.dma_start(out=out_rows[rows, : D // 2], in_=first)
+            nc.sync.dma_start(out=out_rows[rows, D // 2 :], in_=second)
 
         def square_tokens(i):
             x_rms[i] = root_mean_square(x_raw[i][:])
 
-        def scale_tokens_by_rms(i):
-            x_rstd[i] = invert(x_rms[i])
-            scale_tokens(i)
-
         ctx.enter_context(tc.manual_schedule())
         spread_fn_w()
-        load_tokens(0)
-        load_chunk(0)
-        load_tokens(1)
-        load_chunk(1)
-        load_tokens(2)
-        square_tokens(0)
-        transpose_weights(0)
-        transpose_weights(1)
-        x_rstd[0] = invert(x_rms[0])
-        transpose_weights(2)
-        square_tokens(1)
-        transpose_weights(3)
-        scale_tokens(0)
-        quantise_weights(0)
-        for r in range(1, CHUNKS):
-            if r + 1 < CHUNKS:
-                load_chunk(r + 1)
-                if r == 1:
-                    nc.sync.dma_start(out=bias_bc[:], in_=Wk_b.partition_broadcast(P))
-            load_tokens(r + 2)
-            first = r * W_TILES_PER_CHUNK
-            transpose_weights(first)
-            transpose_weights(first + 1)
-            transpose_tokens(r - 1)
-            interleave_tokens(r - 1)
-            scale_tokens_by_rms(r)
-            quantise_tokens(r - 1)
-            transpose_weights(first + 2)
-            square_tokens(r + 1)
-            transpose_weights(first + 3)
-            quantise_weights(r)
-            for i, j in EARLY_PRODUCTS.get(r, ()):
-                multiply(i, j)
-        load_tokens(CHUNKS + 2)
-        nc.sync.dma_start(out=kn_bc[:], in_=kn_w.partition_broadcast(P))
-        transpose_tokens(CHUNKS - 1)
-        interleave_tokens(CHUNKS - 1)
-        scale_tokens_by_rms(CHUNKS)
-        quantise_tokens(CHUNKS - 1)
-        square_tokens(CHUNKS + 1)
-        early = [product for run in EARLY_PRODUCTS.values() for product in run]
+        for n in range(W_TILES):
+            i, q = divmod(n, W_TILES_PER_CHUNK)
+            if q == 0:
+                if i < EARLY:
+                    load_tokens(i)
+                for m in range(n, n + W_TILES_PER_CHUNK):
+                    load_weights(m)
+                if i < EARLY:
+                    square_tokens(i)
+            if q == 1 and i < EARLY:
+                x_rstd[i] = invert(x_rms[i])
+                scale_tokens(i)
+            transpose_weights(n)
+            if q == 3 and i < EARLY:
+                transpose_tokens(i)
+                interleave_tokens(i)
+            if q == 0 and i > 0:
+                quantise_weights(i - 1)
+            if q == 1 and 0 < i <= EARLY:
+                quantise_tokens(i - 1)
+        quantise_weights(CHUNKS - 1)
+        load_tokens(EARLY)
+        load_tokens(EARLY + 1)
+        nc.sync.dma_start(out=bias_bc[:], in_=Wk_b.partition_broadcast(P))
+        nc.sync.dma_start(out=kn_bc[:], in_=kn_w[D // 2 :].partition_broadcast(P))
+        kn_bank = spread_kn_w()
+        for i in range(EARLY + 2, TOKEN_TILES):
+            load_tokens(i)
+        square_tokens(EARLY)
+        square_tokens(EARLY + 1)
+        x_rstd[EARLY] = invert(x_rms[EARLY])
+        scale_tokens(EARLY)
         for s in range(TOKEN_TILES):
-            ahead = s + CHUNKS
-            if ahead + 3 < TOKEN_TILES:
-                load_tokens(ahead + 3)
+            ahead = s + EARLY
             if ahead + 2 < TOKEN_TILES:
                 square_tokens(ahead + 2)
-            left = [j for j in range(CHUNKS) if (s, j) not in early]
-            for j in left:
-                if j == left[-1]:
+            for j in range(CHUNKS):
+                if j == CHUNKS - 1:
                     if s > 0:
                         k_rstd[s - 1] = invert(k_rms[s - 1])
                     if ahead + 1 < TOKEN_TILES:
@@ -280,6 +270,7 @@ def tile_crossattention_pa_kernel(tc, features, fn_w, Wk_w, Wk_b, kn_w, out):
                 scale_tokens(ahead + 1)
             if ahead < TOKEN_TILES:
                 quantise_tokens(ahead)
+            gain_second_half(s)
             k_rms[s] = root_mean_square(k_tiles[s][:])
         k_rstd[TOKEN_TILES - 1] = invert(k_rms[TOKEN_TILES - 1])
         finish(TOKEN_TILES - 1)

@@ -40,7 +40,7 @@ def tile_crossattention_pa_kernel(tc, features, fn_w, Wk_w, Wk_b, kn_w, out):
         x_in = ctx.enter_context(tc.tile_pool(name="x_in", bufs=6))
         w_in = ctx.enter_context(tc.tile_pool(name="w_in", bufs=8))
         work = ctx.enter_context(tc.tile_pool(name="work", bufs=2))
-        stats = ctx.enter_context(tc.tile_pool(name="stats", bufs=2 * TOKEN_TILES))
+        stats = ctx.enter_context(tc.tile_pool(name="stats", bufs=4 * TOKEN_TILES))
         junk_pool = ctx.enter_context(tc.tile_pool(name="junk_pool", bufs=1))
         gained_pool = ctx.enter_context(tc.tile_pool(name="gained_pool", bufs=3))
         k_pool = ctx.enter_context(tc.tile_pool(name="k_pool", bufs=4))
@@ -91,6 +91,7 @@ def tile_crossattention_pa_kernel(tc, features, fn_w, Wk_w, Wk_b, kn_w, out):
         x_banks = {}
         x_grouped = {}
         w_grouped = {}
+        k_meansq = {}
         k_rms = {}
         k_rstd = {}
         w_raw = {}
@@ -104,13 +105,13 @@ def tile_crossattention_pa_kernel(tc, features, fn_w, Wk_w, Wk_b, kn_w, out):
             w_raw[n] = w_in.tile([P, D], BF16, name="w_raw")
             nc.sync.dma_start(out=w_raw[n][:], in_=Wk_w[n * P : (n + 1) * P, :])
 
-        def root_mean_square(values):
+        def add_mean_square(values, before, func):
             junk = junk_pool.tile([P, D], BF16, name="junk")
             sumsq = stats.tile([P, 1], F32, name="sumsq")
-            nc.scalar.activation(out=junk[:], in_=values, func=ACT.Square, accum_out=sumsq[:])
-            rms = stats.tile([P, 1], F32, name="rms")
-            nc.scalar.activation(out=rms[:], in_=sumsq[:], func=ACT.Sqrt, scale=1.0 / D, bias=eps[:])
-            return rms
+            nc.scalar.activation(out=junk[:, : values.shape[1]], in_=values, func=ACT.Square, accum_out=sumsq[:])
+            after = stats.tile([P, 1], F32, name="after")
+            nc.scalar.activation(out=after[:], in_=sumsq[:], func=func, scale=1.0 / D, bias=before[:])
+            return after
 
         def invert(rms):
             rstd = stats.tile([P, 1], F32, name="rstd")
@@ -199,22 +200,30 @@ def tile_crossattention_pa_kernel(tc, features, fn_w, Wk_w, Wk_b, kn_w, out):
             cols = slice(j * CHUNK, (j + 1) * CHUNK)
             nc.vector.tensor_tensor(out=k_tiles[i][:, cols], in0=acc[:], in1=bias_bc[:, cols], op=ALU.add)
 
-        def gain_second_half(i):
-            k_gained[i] = gained_pool.tile([P, D // 2], F32, name="gained")
-            nc.gpsimd.tensor_tensor(out=k_gained[i][:], in0=k_tiles[i][:, D // 2 :], in1=kn_bc[:], op=ALU.mult)
+        def gain(i, j):
+            if i not in k_gained:
+                k_gained[i] = gained_pool.tile([P, D // 2], F32, name="gained")
+            cols = slice((j - 2) * CHUNK, (j - 1) * CHUNK)
+            nc.gpsimd.tensor_tensor(
+                out=k_gained[i][:, cols], in0=k_tiles[i][:, j * CHUNK : (j + 1) * CHUNK], in1=kn_bc[:, cols], op=ALU.mult
+            )
 
         def finish(i):
-            first, second = k_tiles[i][:, : D // 2], k_gained[i][:]
             rows = slice(i * P, (i + 1) * P)
-            nc.scalar.activation(out=second, in_=second, func=ACT.Copy, scale=k_rstd[i][:])
-            nc.vector.scalar_tensor_tensor(
-                out=first, in0=first, scalar=k_rstd[i][:], in1=kn_bank[:], op0=ALU.mult, op1=ALU.mult
-            )
-            nc.sync.dma_start(out=out_rows[rows, : D // 2], in_=first)
-            nc.sync.dma_start(out=out_rows[rows, D // 2 :], in_=second)
+            width = D // 2 if i + 1 < TOKEN_TILES else CHUNK
+            for first in range(0, D // 2, width):
+                cols = slice(first, first + width)
+                gained = k_gained[i][:, cols]
+                nc.scalar.activation(out=gained, in_=gained, func=ACT.Copy, scale=k_rstd[i][:])
+                rest = k_tiles[i][:, cols]
+                nc.vector.scalar_tensor_tensor(
+                    out=rest, in0=rest, scalar=k_rstd[i][:], in1=kn_bank[:, cols], op0=ALU.mult, op1=ALU.mult
+                )
+                nc.sync.dma_start(out=out_rows[rows, cols], in_=rest)
+                nc.sync.dma_start(out=out_rows[rows, D // 2 + first : D // 2 + first + width], in_=gained)
 
         def square_tokens(i):
-            x_rms[i] = root_mean_square(x_raw[i][:])
+            x_rms[i] = add_mean_square(x_raw[i][:], eps, ACT.Sqrt)
 
         ctx.enter_context(tc.manual_schedule())
         spread_fn_w()
@@ -254,13 +263,18 @@ def tile_crossattention_pa_kernel(tc, features, fn_w, Wk_w, Wk_b, kn_w, out):
             ahead = s + EARLY
             if ahead + 2 < TOKEN_TILES:
                 square_tokens(ahead + 2)
-            for j in range(CHUNKS):
-                if j == CHUNKS - 1:
-                    if s > 0:
-                        k_rstd[s - 1] = invert(k_rms[s - 1])
-                    if ahead + 1 < TOKEN_TILES:
-                        x_rstd[ahead + 1] = invert(x_rms[ahead + 1])
+            for j in (2, 3):
                 multiply(s, j)
+                gain(s, j)
+            k_meansq[s] = add_mean_square(k_tiles[s][:, D // 2 :], eps, ACT.Identity)
+            multiply(s, 0)
+            if s + 1 == TOKEN_TILES:
+                k_meansq[s] = add_mean_square(k_tiles[s][:, :CHUNK], k_meansq[s], ACT.Identity)
+            if s > 0:
+                k_rstd[s - 1] = invert(k_rms[s - 1])
+            if ahead + 1 < TOKEN_TILES:
+                x_rstd[ahead + 1] = invert(x_rms[ahead + 1])
+            multiply(s, 1)
             if ahead < TOKEN_TILES:
                 transpose_tokens(ahead)
                 interleave_tokens(ahead)
@@ -270,7 +284,7 @@ def tile_crossattention_pa_kernel(tc, features, fn_w, Wk_w, Wk_b, kn_w, out):
                 scale_tokens(ahead + 1)
             if ahead < TOKEN_TILES:
                 quantise_tokens(ahead)
-            gain_second_half(s)
-            k_rms[s] = root_mean_square(k_tiles[s][:])
+            first = CHUNK if s + 1 == TOKEN_TILES else 0
+            k_rms[s] = add_mean_square(k_tiles[s][:, first : D // 2], k_meansq[s], ACT.Sqrt)
         k_rstd[TOKEN_TILES - 1] = invert(k_rms[TOKEN_TILES - 1])
         finish(TOKEN_TILES - 1)

@@ -53,31 +53,26 @@ def tile_crossattention_pa_kernel(tc, features, fn_w, Wk_w, Wk_b, kn_w, out):
         ident = const.tile([P, P], F32)
         make_identity(nc, ident[:])
 
-        fn_bc = const.tile([P, D], BF16)
         bias_bc = const.tile([P, D], BF16)
         kn_bc = const.tile([P, D // 2], BF16)
         fn_loaded = const.tile([1, D], BF16)
         nc.sync.dma_start(out=fn_loaded[:], in_=fn_w.unsqueeze(0))
         row = const.tile([P, D], BF16)
         nc.vector.memset(row[:].bitcast(I32), 0)
-        nc.vector.tensor_copy(out=row[0:1, :], in_=fn_loaded[:])
+        nc.vector.tensor_copy(
+            out=row[0:1, :].rearrange("p (u w e) -> p u w e", u=2, e=2),
+            in_=fn_loaded[:].rearrange("p (w u e) -> p u w e", u=2, e=2),
+        )
         ones = const.tile([P, P], BF16)
         nc.vector.memset(ones[:], 1.0)
 
-        def spread_fn_w():
-            for j in range(CHUNKS):
-                cols = slice(j * CHUNK, (j + 1) * CHUNK)
-                bank = psum.tile([P, CHUNK], F32, tag="bank")
-                nc.tensor.matmul(out=bank[:], lhsT=ones[:], rhs=row[:, cols], start=True, stop=True)
-                nc.vector.tensor_copy(out=fn_bc[:, cols], in_=bank[:])
-
-        def spread_kn_w():
-            nc.sync.dma_start(out=row[0:1, :], in_=kn_w.unsqueeze(0))
-            kn_bank = psum.tile([P, D // 2], BF16, tag="bank", name="kn_bank")
+        def spread(first):
+            bank = psum.tile([P, D // 2], BF16, tag="bank", name="spread_bank")
             for part in range(2):
                 cols = slice(part * CHUNK, (part + 1) * CHUNK)
-                nc.tensor.matmul(out=kn_bank[:, cols], lhsT=ones[:], rhs=row[:, cols], start=True, stop=True)
-            return kn_bank
+                rhs = row[:, first + part * CHUNK : first + (part + 1) * CHUNK]
+                nc.tensor.matmul(out=bank[:, cols], lhsT=ones[:], rhs=rhs, start=True, stop=True)
+            return bank
 
         x_codes = keep.tile([P, TOKEN_TILES, PASSES * P], U32, align_bytes=64)
         x_scales = keep.tile([P, TOKEN_TILES, PASSES * P], U8, align_bytes=64)
@@ -91,7 +86,6 @@ def tile_crossattention_pa_kernel(tc, features, fn_w, Wk_w, Wk_b, kn_w, out):
         x_banks = {}
         x_grouped = {}
         w_grouped = {}
-        k_meansq = {}
         k_rms = {}
         k_rstd = {}
         w_raw = {}
@@ -135,13 +129,12 @@ def tile_crossattention_pa_kernel(tc, features, fn_w, Wk_w, Wk_b, kn_w, out):
         def scale_tokens(i):
             x_n[i] = work.tile([P, 2, D // 2], BF16, name="x_n")
             x_pairs = x_raw[i][:].rearrange("p (w u e) -> p u w e", u=2, e=2)
-            fn_pairs = fn_bc[:].rearrange("p (w u e) -> p u w e", u=2, e=2)
             for u in range(2):
                 nc.vector.scalar_tensor_tensor(
                     out=x_n[i][:, u, :].rearrange("p (w e) -> p w e", e=2),
                     in0=x_pairs[:, u],
                     scalar=x_rstd[i][:],
-                    in1=fn_pairs[:, u],
+                    in1=fn_banks[u][:].rearrange("p (w e) -> p w e", e=2),
                     op0=ALU.mult,
                     op1=ALU.mult,
                 )
@@ -226,7 +219,7 @@ def tile_crossattention_pa_kernel(tc, features, fn_w, Wk_w, Wk_b, kn_w, out):
             x_rms[i] = add_mean_square(x_raw[i][:], eps, ACT.Sqrt)
 
         ctx.enter_context(tc.manual_schedule())
-        spread_fn_w()
+        fn_banks = [spread(u * D // 2) for u in range(2)]
         for n in range(W_TILES):
             i, q = divmod(n, W_TILES_PER_CHUNK)
             if q == 0:
@@ -252,7 +245,8 @@ def tile_crossattention_pa_kernel(tc, features, fn_w, Wk_w, Wk_b, kn_w, out):
         load_tokens(EARLY + 1)
         nc.sync.dma_start(out=bias_bc[:], in_=Wk_b.partition_broadcast(P))
         nc.sync.dma_start(out=kn_bc[:], in_=kn_w[D // 2 :].partition_broadcast(P))
-        kn_bank = spread_kn_w()
+        nc.sync.dma_start(out=row[0:1, :], in_=kn_w.unsqueeze(0))
+        kn_bank = spread(0)
         for i in range(EARLY + 2, TOKEN_TILES):
             load_tokens(i)
         square_tokens(EARLY)
@@ -263,13 +257,15 @@ def tile_crossattention_pa_kernel(tc, features, fn_w, Wk_w, Wk_b, kn_w, out):
             ahead = s + EARLY
             if ahead + 2 < TOKEN_TILES:
                 square_tokens(ahead + 2)
+            last = s + 1 == TOKEN_TILES
             for j in (2, 3):
                 multiply(s, j)
                 gain(s, j)
-            k_meansq[s] = add_mean_square(k_tiles[s][:, D // 2 :], eps, ACT.Identity)
+            if last:
+                k_meansq = add_mean_square(k_tiles[s][:, D // 2 :], eps, ACT.Identity)
             multiply(s, 0)
-            if s + 1 == TOKEN_TILES:
-                k_meansq[s] = add_mean_square(k_tiles[s][:, :CHUNK], k_meansq[s], ACT.Identity)
+            if last:
+                k_meansq = add_mean_square(k_tiles[s][:, :CHUNK], k_meansq, ACT.Identity)
             if s > 0:
                 k_rstd[s - 1] = invert(k_rms[s - 1])
             if ahead + 1 < TOKEN_TILES:
@@ -278,13 +274,15 @@ def tile_crossattention_pa_kernel(tc, features, fn_w, Wk_w, Wk_b, kn_w, out):
             if ahead < TOKEN_TILES:
                 transpose_tokens(ahead)
                 interleave_tokens(ahead)
+            if last:
+                k_rms[s] = add_mean_square(k_tiles[s][:, CHUNK : D // 2], k_meansq, ACT.Sqrt)
             if s > 0:
                 finish(s - 1)
             if ahead + 1 < TOKEN_TILES:
                 scale_tokens(ahead + 1)
             if ahead < TOKEN_TILES:
                 quantise_tokens(ahead)
-            first = CHUNK if s + 1 == TOKEN_TILES else 0
-            k_rms[s] = add_mean_square(k_tiles[s][:, first : D // 2], k_meansq[s], ACT.Sqrt)
+            if not last:
+                k_rms[s] = add_mean_square(k_tiles[s][:], eps, ACT.Sqrt)
         k_rstd[TOKEN_TILES - 1] = invert(k_rms[TOKEN_TILES - 1])
         finish(TOKEN_TILES - 1)

@@ -24,7 +24,10 @@ CHUNKS = D // CHUNK
 W_TILES_PER_CHUNK = CHUNK // P
 TOKEN_TILES = TOKENS // P
 W_TILES = D // P
+W_BUFS = 8
 EARLY = 3
+LOAD_AT = (0, 2, 6)
+SQUARE_AT = (0, 2, 5)
 
 FLOPS = 2 * TOKENS * D * D
 
@@ -38,7 +41,7 @@ def tile_crossattention_pa_kernel(tc, features, fn_w, Wk_w, Wk_b, kn_w, out):
         const = ctx.enter_context(tc.tile_pool(name="const", bufs=1))
         keep = ctx.enter_context(tc.tile_pool(name="keep", bufs=1))
         x_in = ctx.enter_context(tc.tile_pool(name="x_in", bufs=6))
-        w_in = ctx.enter_context(tc.tile_pool(name="w_in", bufs=8))
+        w_in = ctx.enter_context(tc.tile_pool(name="w_in", bufs=W_BUFS))
         work = ctx.enter_context(tc.tile_pool(name="work", bufs=2))
         stats = ctx.enter_context(tc.tile_pool(name="stats", bufs=4 * TOKEN_TILES))
         junk_pool = ctx.enter_context(tc.tile_pool(name="junk_pool", bufs=1))
@@ -59,10 +62,7 @@ def tile_crossattention_pa_kernel(tc, features, fn_w, Wk_w, Wk_b, kn_w, out):
         nc.sync.dma_start(out=fn_loaded[:], in_=fn_w.unsqueeze(0))
         row = const.tile([P, D], BF16)
         nc.vector.memset(row[:].bitcast(I32), 0)
-        nc.vector.tensor_copy(
-            out=row[0:1, :].rearrange("p (u w e) -> p u w e", u=2, e=2),
-            in_=fn_loaded[:].rearrange("p (w u e) -> p u w e", u=2, e=2),
-        )
+        nc.vector.tensor_copy(out=row[0:1, :], in_=fn_loaded[:])
         ones = const.tile([P, P], BF16)
         nc.vector.memset(ones[:], 1.0)
 
@@ -127,21 +127,21 @@ def tile_crossattention_pa_kernel(tc, features, fn_w, Wk_w, Wk_b, kn_w, out):
                 copies[half](out=grouped_of(half), in_=banks[half][:].rearrange("p c u r -> p c r u"))
 
         def scale_tokens(i):
-            x_n[i] = work.tile([P, 2, D // 2], BF16, name="x_n")
-            x_pairs = x_raw[i][:].rearrange("p (w u e) -> p u w e", u=2, e=2)
-            for u in range(2):
+            x_n[i] = work.tile([P, D], BF16, name="x_n")
+            for half in range(2):
+                cols = slice(half * D // 2, (half + 1) * D // 2)
                 nc.vector.scalar_tensor_tensor(
-                    out=x_n[i][:, u, :].rearrange("p (w e) -> p w e", e=2),
-                    in0=x_pairs[:, u],
+                    out=x_n[i][:, cols],
+                    in0=x_raw[i][:, cols],
                     scalar=x_rstd[i][:],
-                    in1=fn_banks[u][:].rearrange("p (w e) -> p w e", e=2),
+                    in1=fn_banks[half][:],
                     op0=ALU.mult,
                     op1=ALU.mult,
                 )
 
         def transpose_tokens(i):
-            words = x_n[i][:].rearrange("p u w -> p (u w)").bitcast(F32)
-            x_banks[i] = transpose_words(lambda c, u: words[:, (u * PASSES + c) * P : (u * PASSES + c + 1) * P])
+            words = x_n[i][:].bitcast(F32)
+            x_banks[i] = transpose_words(lambda c, u: words[:, 2 * P * c + u : 2 * P * (c + 1) : 2])
 
         def interleave_tokens(i):
             x_grouped[i] = work.tile([P, D], BF16, name="x_grouped", align_bytes=64)
@@ -163,7 +163,7 @@ def tile_crossattention_pa_kernel(tc, features, fn_w, Wk_w, Wk_b, kn_w, out):
             copies = [nc.scalar.copy, nc.scalar.copy]
             if j == 0:
                 copies[n % 2] = nc.vector.tensor_copy
-            elif n % 2 == 1:
+            elif n % 2 == 0:
                 copies[1] = nc.vector.tensor_copy
             interleave(banks, copies, lambda half: grouped[:, 2 * half : 2 * half + 2, m])
 
@@ -207,7 +207,12 @@ def tile_crossattention_pa_kernel(tc, features, fn_w, Wk_w, Wk_b, kn_w, out):
             for first in range(0, D // 2, width):
                 cols = slice(first, first + width)
                 gained = k_gained[i][:, cols]
-                nc.scalar.activation(out=gained, in_=gained, func=ACT.Copy, scale=k_rstd[i][:])
+                if i + 1 < TOKEN_TILES:
+                    nc.gpsimd.tensor_scalar(
+                        out=gained, in0=gained, scalar1=k_rstd[i][:], scalar2=0.0, op0=ALU.mult, op1=ALU.add
+                    )
+                else:
+                    nc.scalar.activation(out=gained, in_=gained, func=ACT.Copy, scale=k_rstd[i][:])
                 rest = k_tiles[i][:, cols]
                 nc.vector.scalar_tensor_tensor(
                     out=rest, in0=rest, scalar=k_rstd[i][:], in1=kn_bank[:, cols], op0=ALU.mult, op1=ALU.mult
@@ -218,41 +223,47 @@ def tile_crossattention_pa_kernel(tc, features, fn_w, Wk_w, Wk_b, kn_w, out):
         def square_tokens(i):
             x_rms[i] = add_mean_square(x_raw[i][:], eps, ACT.Sqrt)
 
+        def load(n):
+            if n in LOAD_AT:
+                load_tokens(LOAD_AT.index(n))
+            load_weights(n)
+
         ctx.enter_context(tc.manual_schedule())
         fn_banks = [spread(u * D // 2) for u in range(2)]
+        for n in range(W_BUFS):
+            load(n)
         for n in range(W_TILES):
-            i, q = divmod(n, W_TILES_PER_CHUNK)
-            if q == 0:
-                if i < EARLY:
-                    load_tokens(i)
-                for m in range(n, n + W_TILES_PER_CHUNK):
-                    load_weights(m)
-                if i < EARLY:
+            for i in range(EARLY):
+                if n == SQUARE_AT[i]:
                     square_tokens(i)
-            if q == 1 and i < EARLY:
-                x_rstd[i] = invert(x_rms[i])
-                scale_tokens(i)
+                if n == SQUARE_AT[i] + 1:
+                    x_rstd[i] = invert(x_rms[i])
+                    scale_tokens(i)
             transpose_weights(n)
-            if q == 3 and i < EARLY:
-                transpose_tokens(i)
-                interleave_tokens(i)
-            if q == 0 and i > 0:
-                quantise_weights(i - 1)
-            if q == 1 and 0 < i <= EARLY:
-                quantise_tokens(i - 1)
+            if n + W_BUFS < W_TILES:
+                load(n + W_BUFS)
+            for i in range(EARLY):
+                if n == SQUARE_AT[i] + 3:
+                    transpose_tokens(i)
+                    interleave_tokens(i)
+            if n > 0 and n % W_TILES_PER_CHUNK == 0:
+                quantise_weights(n // W_TILES_PER_CHUNK - 1)
+            for i in range(EARLY):
+                if n == SQUARE_AT[i] + 4:
+                    quantise_tokens(i)
         quantise_weights(CHUNKS - 1)
         load_tokens(EARLY)
         load_tokens(EARLY + 1)
         nc.sync.dma_start(out=bias_bc[:], in_=Wk_b.partition_broadcast(P))
         nc.sync.dma_start(out=kn_bc[:], in_=kn_w[D // 2 :].partition_broadcast(P))
         nc.sync.dma_start(out=row[0:1, :], in_=kn_w.unsqueeze(0))
-        kn_bank = spread(0)
         for i in range(EARLY + 2, TOKEN_TILES):
             load_tokens(i)
         square_tokens(EARLY)
         square_tokens(EARLY + 1)
         x_rstd[EARLY] = invert(x_rms[EARLY])
         scale_tokens(EARLY)
+        kn_bank = spread(0)
         for s in range(TOKEN_TILES):
             ahead = s + EARLY
             if ahead + 2 < TOKEN_TILES:

from contextlib import ExitStack

import concourse.mybir as mybir
from concourse.masks import make_identity

F32 = mybir.dt.float32
BF16 = mybir.dt.bfloat16
U32 = mybir.dt.uint32
U8 = mybir.dt.uint8
I32 = mybir.dt.int32
FP8X4 = mybir.dt.float8_e4m3fn_x4
ALU = mybir.AluOpType
ACT = mybir.ActivationFunctionType

P = 128
TOKENS = 1024
D = 2048
EPS = 1e-6
PACK = 4
K_PASS = P * PACK
PASSES = D // K_PASS
CHUNK = 512
CHUNKS = D // CHUNK
W_TILES_PER_CHUNK = CHUNK // P
TOKEN_TILES = TOKENS // P
W_TILES = D // P
W_BUFS = 8
EARLY = 3
LOAD_AT = (0, 2, 6)
SQUARE_AT = (0, 2, 5)

FLOPS = 2 * TOKENS * D * D


def tile_crossattention_pa_kernel(tc, features, fn_w, Wk_w, Wk_b, kn_w, out):
    nc = tc.nc
    x_rows = features.flatten_outer_dims()
    out_rows = out.flatten_outer_dims()

    with ExitStack() as ctx:
        const = ctx.enter_context(tc.tile_pool(name="const", bufs=1))
        keep = ctx.enter_context(tc.tile_pool(name="keep", bufs=1))
        x_in = ctx.enter_context(tc.tile_pool(name="x_in", bufs=6))
        w_in = ctx.enter_context(tc.tile_pool(name="w_in", bufs=W_BUFS))
        work = ctx.enter_context(tc.tile_pool(name="work", bufs=2))
        stats = ctx.enter_context(tc.tile_pool(name="stats", bufs=4 * TOKEN_TILES))
        junk_pool = ctx.enter_context(tc.tile_pool(name="junk_pool", bufs=1))
        gained_pool = ctx.enter_context(tc.tile_pool(name="gained_pool", bufs=3))
        k_pool = ctx.enter_context(tc.tile_pool(name="k_pool", bufs=4))
        psum = ctx.enter_context(tc.psum_pool(name="psum", bufs=8))

        eps = const.tile([P, 1], F32)
        nc.vector.memset(eps[:], EPS)
        warm = const.tile([P, 1], F32)
        nc.scalar.activation(out=warm[:], in_=eps[:], func=ACT.Sqrt)
        ident = const.tile([P, P], F32)
        make_identity(nc, ident[:])

        bias_bc = const.tile([P, D], BF16)
        kn_bc = const.tile([P, D // 2], BF16)
        fn_loaded = const.tile([1, D], BF16)
        nc.sync.dma_start(out=fn_loaded[:], in_=fn_w.unsqueeze(0))
        row = const.tile([P, D], BF16)
        nc.vector.memset(row[:].bitcast(I32), 0)
        nc.vector.tensor_copy(out=row[0:1, :], in_=fn_loaded[:])
        ones = const.tile([P, P], BF16)
        nc.vector.memset(ones[:], 1.0)

        def spread(first):
            bank = psum.tile([P, D // 2], BF16, tag="bank", name="spread_bank")
            for part in range(2):
                cols = slice(part * CHUNK, (part + 1) * CHUNK)
                rhs = row[:, first + part * CHUNK : first + (part + 1) * CHUNK]
                nc.tensor.matmul(out=bank[:, cols], lhsT=ones[:], rhs=rhs, start=True, stop=True)
            return bank

        x_codes = keep.tile([P, TOKEN_TILES, PASSES * P], U32, align_bytes=64)
        x_scales = keep.tile([P, TOKEN_TILES, PASSES * P], U8, align_bytes=64)
        w_codes = keep.tile([P, CHUNKS, PASSES * CHUNK], U32, align_bytes=64)
        w_scales = keep.tile([P, CHUNKS, PASSES * CHUNK], U8, align_bytes=64)
        k_gained = {}
        x_raw = {}
        x_rms = {}
        x_rstd = {}
        x_n = {}
        x_banks = {}
        x_grouped = {}
        w_grouped = {}
        k_rms = {}
        k_rstd = {}
        w_raw = {}
        k_tiles = {}

        def load_tokens(i):
            x_raw[i] = x_in.tile([P, D], BF16, name="x_raw")
            nc.sync.dma_start(out=x_raw[i][:], in_=x_rows[i * P : (i + 1) * P, :])

        def load_weights(n):
            w_raw[n] = w_in.tile([P, D], BF16, name="w_raw")
            nc.sync.dma_start(out=w_raw[n][:], in_=Wk_w[n * P : (n + 1) * P, :])

        def add_mean_square(values, before, func):
            junk = junk_pool.tile([P, D], BF16, name="junk")
            sumsq = stats.tile([P, 1], F32, name="sumsq")
            nc.scalar.activation(out=junk[:, : values.shape[1]], in_=values, func=ACT.Square, accum_out=sumsq[:])
            after = stats.tile([P, 1], F32, name="after")
            nc.scalar.activation(out=after[:], in_=sumsq[:], func=func, scale=1.0 / D, bias=before[:])
            return after

        def invert(rms):
            rstd = stats.tile([P, 1], F32, name="rstd")
            nc.vector.reciprocal(out=rstd[:], in_=rms[:])
            return rstd

        def transpose_words(words_of):
            banks = []
            for half in range(2):
                bank = psum.tile([P, 2, 2, P], F32, tag="bank", name="bank")
                for c2 in range(2):
                    for u in range(2):
                        nc.tensor.transpose(bank[:, c2, u, :], words_of(2 * half + c2, u), ident[:])
                banks.append(bank)
            return banks

        def interleave(banks, copies, grouped_of):
            for half in range(2):
                copies[half](out=grouped_of(half), in_=banks[half][:].rearrange("p c u r -> p c r u"))

        def scale_tokens(i):
            x_n[i] = work.tile([P, D], BF16, name="x_n")
            for half in range(2):
                cols = slice(half * D // 2, (half + 1) * D // 2)
                nc.vector.scalar_tensor_tensor(
                    out=x_n[i][:, cols],
                    in0=x_raw[i][:, cols],
                    scalar=x_rstd[i][:],
                    in1=fn_banks[half][:],
                    op0=ALU.mult,
                    op1=ALU.mult,
                )

        def transpose_tokens(i):
            words = x_n[i][:].bitcast(F32)
            x_banks[i] = transpose_words(lambda c, u: words[:, 2 * P * c + u : 2 * P * (c + 1) : 2])

        def interleave_tokens(i):
            x_grouped[i] = work.tile([P, D], BF16, name="x_grouped", align_bytes=64)
            grouped = x_grouped[i][:].bitcast(F32).rearrange("p (c r u) -> p c r u", c=PASSES, r=P, u=2)
            interleave(x_banks[i], (nc.scalar.copy, nc.scalar.copy), lambda half: grouped[:, 2 * half : 2 * half + 2])

        def quantise_tokens(i):
            nc.vector.quantize_mx(out=x_codes[:, i, :].bitcast(FP8X4), scales=x_scales[:, i, :], in_=x_grouped[i][:])

        def transpose_weights(n):
            j, m = divmod(n, W_TILES_PER_CHUNK)
            if m == 0:
                w_grouped[j] = work.tile([P, PASSES * CHUNK * PACK], BF16, name="w_grouped", align_bytes=64)
            grouped = w_grouped[j][:].bitcast(F32).rearrange(
                "p (c n r u) -> p c n r u", c=PASSES, n=W_TILES_PER_CHUNK, r=P, u=2
            )
            words = w_raw[n][:].bitcast(F32)
            banks = transpose_words(lambda c, u: words[:, 2 * P * c + u : 2 * P * (c + 1) : 2])
            copies = [nc.scalar.copy, nc.scalar.copy]
            if j == 0:
                copies[n % 2] = nc.vector.tensor_copy
            elif n % 2 == 0:
                copies[1] = nc.vector.tensor_copy
            interleave(banks, copies, lambda half: grouped[:, 2 * half : 2 * half + 2, m])

        def quantise_weights(j):
            for half in range(2):
                cols = slice(half * 2 * CHUNK, (half + 1) * 2 * CHUNK)
                nc.vector.quantize_mx(
                    out=w_codes[:, j, cols].bitcast(FP8X4),
                    scales=w_scales[:, j, cols],
                    in_=w_grouped[j][:, half * 2 * CHUNK * PACK : (half + 1) * 2 * CHUNK * PACK],
                )

        def multiply(i, j):
            if i not in k_tiles:
                k_tiles[i] = k_pool.tile([P, D], F32, name="k_tile")
            acc = psum.tile([P, CHUNK], F32, tag="bank")
            for c in range(PASSES):
                nc.tensor.matmul_mx(
                    out=acc[:],
                    lhsT=x_codes[:, i, c * P : (c + 1) * P].bitcast(FP8X4),
                    lhsT_scale=x_scales[:, i, c * P : (c + 1) * P],
                    rhs=w_codes[:, j, c * CHUNK : (c + 1) * CHUNK].bitcast(FP8X4),
                    rhs_scale=w_scales[:, j, c * CHUNK : (c + 1) * CHUNK],
                    start=(c == 0),
                    stop=(c == PASSES - 1),
                )
            cols = slice(j * CHUNK, (j + 1) * CHUNK)
            nc.vector.tensor_tensor(out=k_tiles[i][:, cols], in0=acc[:], in1=bias_bc[:, cols], op=ALU.add)

        def gain(i, j):
            if i not in k_gained:
                k_gained[i] = gained_pool.tile([P, D // 2], F32, name="gained")
            cols = slice((j - 2) * CHUNK, (j - 1) * CHUNK)
            nc.gpsimd.tensor_tensor(
                out=k_gained[i][:, cols], in0=k_tiles[i][:, j * CHUNK : (j + 1) * CHUNK], in1=kn_bc[:, cols], op=ALU.mult
            )

        def finish(i):
            rows = slice(i * P, (i + 1) * P)
            width = D // 2 if i + 1 < TOKEN_TILES else CHUNK
            for first in range(0, D // 2, width):
                cols = slice(first, first + width)
                gained = k_gained[i][:, cols]
                if i + 1 < TOKEN_TILES:
                    nc.gpsimd.tensor_scalar(
                        out=gained, in0=gained, scalar1=k_rstd[i][:], scalar2=0.0, op0=ALU.mult, op1=ALU.add
                    )
                else:
                    nc.scalar.activation(out=gained, in_=gained, func=ACT.Copy, scale=k_rstd[i][:])
                rest = k_tiles[i][:, cols]
                nc.vector.scalar_tensor_tensor(
                    out=rest, in0=rest, scalar=k_rstd[i][:], in1=kn_bank[:, cols], op0=ALU.mult, op1=ALU.mult
                )
                nc.sync.dma_start(out=out_rows[rows, cols], in_=rest)
                nc.sync.dma_start(out=out_rows[rows, D // 2 + first : D // 2 + first + width], in_=gained)

        def square_tokens(i):
            x_rms[i] = add_mean_square(x_raw[i][:], eps, ACT.Sqrt)

        def load(n):
            if n in LOAD_AT:
                load_tokens(LOAD_AT.index(n))
            load_weights(n)

        ctx.enter_context(tc.manual_schedule())
        fn_banks = [spread(u * D // 2) for u in range(2)]
        for n in range(W_BUFS):
            load(n)
        for n in range(W_TILES):
            for i in range(EARLY):
                if n == SQUARE_AT[i]:
                    square_tokens(i)
                if n == SQUARE_AT[i] + 1:
                    x_rstd[i] = invert(x_rms[i])
                    scale_tokens(i)
            transpose_weights(n)
            if n + W_BUFS < W_TILES:
                load(n + W_BUFS)
            for i in range(EARLY):
                if n == SQUARE_AT[i] + 3:
                    transpose_tokens(i)
                    interleave_tokens(i)
            if n > 0 and n % W_TILES_PER_CHUNK == 0:
                quantise_weights(n // W_TILES_PER_CHUNK - 1)
            for i in range(EARLY):
                if n == SQUARE_AT[i] + 4:
                    quantise_tokens(i)
        quantise_weights(CHUNKS - 1)
        load_tokens(EARLY)
        load_tokens(EARLY + 1)
        nc.sync.dma_start(out=bias_bc[:], in_=Wk_b.partition_broadcast(P))
        nc.sync.dma_start(out=kn_bc[:], in_=kn_w[D // 2 :].partition_broadcast(P))
        nc.sync.dma_start(out=row[0:1, :], in_=kn_w.unsqueeze(0))
        for i in range(EARLY + 2, TOKEN_TILES):
            load_tokens(i)
        square_tokens(EARLY)
        square_tokens(EARLY + 1)
        x_rstd[EARLY] = invert(x_rms[EARLY])
        scale_tokens(EARLY)
        kn_bank = spread(0)
        for s in range(TOKEN_TILES):
            ahead = s + EARLY
            if ahead + 2 < TOKEN_TILES:
                square_tokens(ahead + 2)
            last = s + 1 == TOKEN_TILES
            for j in (2, 3):
                multiply(s, j)
                gain(s, j)
            if last:
                k_meansq = add_mean_square(k_tiles[s][:, D // 2 :], eps, ACT.Identity)
            multiply(s, 0)
            if last:
                k_meansq = add_mean_square(k_tiles[s][:, :CHUNK], k_meansq, ACT.Identity)
            if s > 0:
                k_rstd[s - 1] = invert(k_rms[s - 1])
            if ahead + 1 < TOKEN_TILES:
                x_rstd[ahead + 1] = invert(x_rms[ahead + 1])
            multiply(s, 1)
            if ahead < TOKEN_TILES:
                transpose_tokens(ahead)
                interleave_tokens(ahead)
            if last:
                k_rms[s] = add_mean_square(k_tiles[s][:, CHUNK : D // 2], k_meansq, ACT.Sqrt)
            if s > 0:
                finish(s - 1)
            if ahead + 1 < TOKEN_TILES:
                scale_tokens(ahead + 1)
            if ahead < TOKEN_TILES:
                quantise_tokens(ahead)
            if not last:
                k_rms[s] = add_mean_square(k_tiles[s][:], eps, ACT.Sqrt)
        k_rstd[TOKEN_TILES - 1] = invert(k_rms[TOKEN_TILES - 1])
        finish(TOKEN_TILES - 1)
